import numpy as np
import ml_dtypes


def mxq(x, axis, fmt="e4m3"):
    dtype, down = {"e4m3": (ml_dtypes.float8_e4m3fn, 7), "e5m2": (ml_dtypes.float8_e5m2, 14)}[fmt]
    v = np.moveaxis(np.asarray(x, np.float32).astype(ml_dtypes.bfloat16).astype(np.float64), axis, -1)
    blocks = v.reshape(v.shape[:-1] + (-1, 32))
    amax = np.abs(blocks).max(-1, keepdims=True)
    byte = np.maximum(np.where(amax > 0, np.frexp(amax)[1] - 1 + 127, 0) - down, 1)
    scale = np.exp2(byte - 127.0)
    codes = (blocks / scale).astype(np.float32).astype(dtype).astype(np.float64)
    return np.moveaxis((codes * scale).reshape(v.shape), -1, axis)


WIDE = False


def mx_kscale(k):
    if not WIDE:
        return np.ones(k)
    levels = np.array([10, -10, 5, -5, 0])
    a = np.random.permutation(np.resize(levels, k // 512 * 4)).reshape(k // 512, 4)
    idx = np.arange(k)
    return np.exp2(a[idx // 512, idx % 128 // 32])


BF16 = ml_dtypes.bfloat16


def bf(x):
    return np.asarray(x, np.float32).astype(BF16)


def f64(x):
    return np.asarray(x).astype(np.float64)


E2M1 = np.array([0.0, 0.5, 1.0, 1.5, 2.0, 3.0, 4.0, 6.0, -0.0, -0.5, -1.0, -1.5, -2.0, -3.0, -4.0, -6.0])


def pack_weight(w, fmt):
    k, n = w.shape
    w = f64(bf(w)).reshape(k // 32, 32, n)
    amax = np.abs(w).max(1)
    if fmt == "e4m3":
        byte = np.frexp(amax)[1] - 1 + 127 - 7
    else:
        mant, ex = np.frexp(amax / 6.0)
        byte = np.where(mant > 0.5, ex, ex - 1) + 127
    byte = np.clip(np.where(amax > 0, byte, 1), 1, 254)
    scaled = (w * np.exp2(127.0 - byte)[:, None, :]).reshape(k, n).astype(np.float32)
    by_word = np.ascontiguousarray(scaled.reshape(k // 512, 128, 4, n).transpose(0, 1, 3, 2))
    if fmt == "e4m3":
        words = by_word.astype(ml_dtypes.float8_e4m3fn).view(np.uint8)
    else:
        c = by_word.astype(ml_dtypes.float4_e2m1fn).view(np.uint8) & 0xF
        words = c[..., 0::2] | (c[..., 1::2] << 4)
    return np.ascontiguousarray(words), np.ascontiguousarray(byte.astype(np.uint8).reshape(k // 512, 16, n))


def unpack_weight(words, scales, fmt):
    g, p, n, _ = words.shape
    if fmt == "e4m3":
        vals = np.ascontiguousarray(words).view(ml_dtypes.float8_e4m3fn).astype(np.float64)
    else:
        nib = np.empty((g, p, n, 4), np.uint8)
        nib[..., 0::2] = words & 0xF
        nib[..., 1::2] = words >> 4
        vals = E2M1[nib]
    vals = vals * np.repeat(np.exp2(scales.astype(np.float64) - 127.0), 8, axis=1)[..., None]
    return vals.transpose(0, 1, 3, 2).reshape(g * 512, n)


B, S, D, F, R = 2, 128, 16384, 512, 128
SCALING = 2.0
FMT = "e4m3"


def silu(v):
    return v / (1.0 + np.exp(-v))


def setup_inputs():
    s = mx_kscale(D)
    x = bf(np.random.standard_normal((B, S, D)) * s)
    w1 = np.random.standard_normal((F, D)) / np.sqrt(D) / s
    w3 = np.random.standard_normal((F, D)) / np.sqrt(D) / s
    xa1 = bf(np.random.standard_normal((B, S, R)))
    xa3 = bf(np.random.standard_normal((B, S, R)))
    lora_B1 = bf(np.random.standard_normal((F, R)) * 0.25 / np.sqrt(R))
    lora_B3 = bf(np.random.standard_normal((F, R)) * 0.25 / np.sqrt(R))
    lora_A2 = np.random.standard_normal((R, F)) / np.sqrt(F)
    w1_words, w1_scales = pack_weight(np.ascontiguousarray(w1.T), FMT)
    w3_words, w3_scales = pack_weight(np.ascontiguousarray(w3.T), FMT)
    lora_A2_words, lora_A2_scales = pack_weight(np.ascontiguousarray(lora_A2.T), FMT)
    return {
        "x": x,
        "w1_words": w1_words,
        "w1_scales": w1_scales,
        "w3_words": w3_words,
        "w3_scales": w3_scales,
        "xa1": xa1,
        "xa3": xa3,
        "lora_B1": lora_B1,
        "lora_B3": lora_B3,
        "lora_A2_words": lora_A2_words,
        "lora_A2_scales": lora_A2_scales,
    }


def reference(x, w1_words, w1_scales, w3_words, w3_scales, xa1, xa3, lora_B1, lora_B3, lora_A2_words, lora_A2_scales):
    xq = mxq(f64(x), 2, "e4m3")
    h1 = (xq @ unpack_weight(w1_words, w1_scales, FMT)) + (f64(xa1) @ f64(lora_B1).T) * SCALING
    h3 = (xq @ unpack_weight(w3_words, w3_scales, FMT)) + (f64(xa3) @ f64(lora_B3).T) * SCALING
    g = silu(h1) * h3
    ga2 = mxq(g, 2, "e4m3") @ unpack_weight(lora_A2_words, lora_A2_scales, FMT)
    return g, ga2

@@ -1,0 +1,289 @@
+from contextlib import ExitStack
+
+import concourse.mybir as mybir
+from concourse.masks import make_identity
+
+F32 = mybir.dt.float32
+BF16 = mybir.dt.bfloat16
+I32 = mybir.dt.int32
+U32 = mybir.dt.uint32
+U8 = mybir.dt.uint8
+FP8X4 = mybir.dt.float8_e4m3fn_x4
+SILU = mybir.ActivationFunctionType.Silu
+
+P = 128
+TOKEN_TILES = 2
+D = 16384
+F = 512
+R = 128
+PACK = 4
+K_PASS = P * PACK
+CHUNK_GROUPS = 8
+CHUNKS = D // (K_PASS * CHUNK_GROUPS)
+CHUNK_COLS = K_PASS * CHUNK_GROUPS
+PIECE_GROUPS = 2
+PIECES = CHUNK_GROUPS // PIECE_GROUPS
+BANK_GROUPS = 2
+WORDS_PER_GROUP = K_PASS // 2
+LORA_SCALING = 2.0
+
+FLOPS = 2 * TOKEN_TILES * P * (2 * D * F + 2 * R * F + F * R)
+
+
+def tile_feedforward_pa_k_kernel(
+    tc,
+    x,
+    w1_words,
+    w1_scales,
+    w3_words,
+    w3_scales,
+    xa1,
+    xa3,
+    lora_B1,
+    lora_B3,
+    lora_A2_words,
+    lora_A2_scales,
+    out_0,
+    out_1,
+):
+    nc = tc.nc
+    branches = ("w1", "w3")
+    words_of = {"w1": w1_words, "w3": w3_words}
+    scales_of = {"w1": w1_scales, "w3": w3_scales}
+    lora_inputs = {"w1": (xa1, lora_B1), "w3": (xa3, lora_B3)}
+    steps = [(branch, chunk) for branch in branches for chunk in range(CHUNKS)]
+
+    with ExitStack() as ctx:
+        keep = ctx.enter_context(tc.tile_pool(name="keep", bufs=1))
+        x_pool = ctx.enter_context(tc.tile_pool(name="x_pool", bufs=2 * TOKEN_TILES))
+        grouped_pool = ctx.enter_context(tc.tile_pool(name="grouped_pool", bufs=TOKEN_TILES))
+        w_pool = ctx.enter_context(tc.tile_pool(name="w_pool", bufs=3 * PIECES))
+        turn_psum = ctx.enter_context(tc.psum_pool(name="turn_psum", bufs=4))
+        acc_psum = ctx.enter_context(tc.psum_pool(name="acc_psum", bufs=1))
+        ctx.enter_context(tc.manual_schedule())
+
+        planes = {}
+        for branch, chunk in steps:
+            planes[(branch, chunk)] = keep.tile(
+                [P, CHUNK_GROUPS, F], U8, name="planes_%s_%d" % (branch, chunk), align_bytes=64
+            )
+            nc.vector.memset(planes[(branch, chunk)][:].bitcast(I32), 0)
+        a2_plane = keep.tile([P, R], U8, name="a2_plane", align_bytes=64)
+        nc.vector.memset(a2_plane[:].bitcast(I32), 0)
+
+        identity_f32 = keep.tile([P, P], F32, name="identity_f32")
+        make_identity(nc, identity_f32[:])
+        identity_bf16 = keep.tile([P, P], BF16, name="identity_bf16")
+        make_identity(nc, identity_bf16[:])
+
+        for branch, chunk in steps:
+            rows = scales_of[branch].bitcast(F32)[
+                chunk * CHUNK_GROUPS : (chunk + 1) * CHUNK_GROUPS
+            ]
+            for r in range(4):
+                nc.gpsimd.dma_start(
+                    out=planes[(branch, chunk)][4 * chunk + r : P : 32, :, :].bitcast(F32),
+                    in_=rows[:, r : 16 : 4, :].rearrange("g q n -> q g n"),
+                )
+        a2_words = keep.tile([P, R], U32, name="a2_words", align_bytes=64)
+        nc.gpsimd.dma_start(
+            out=a2_words[:].bitcast(F32),
+            in_=lora_A2_words[0].rearrange("p n t -> p (n t)").bitcast(F32),
+        )
+        for r in range(4):
+            nc.gpsimd.dma_start(
+                out=a2_plane[r : P : 32, :].bitcast(F32),
+                in_=lora_A2_scales[0].bitcast(F32)[r : 16 : 4, :],
+            )
+
+        x_raw = {}
+        x_codes = {}
+        x_scales = {}
+        w_pieces = {}
+
+        def load_x(chunk):
+            for tt in range(TOKEN_TILES):
+                raw = x_pool.tile([P, CHUNK_COLS], BF16, name="x_raw", tag="x_raw")
+                nc.sync.dma_start(
+                    out=raw[:], in_=x[tt, :, chunk * CHUNK_COLS : (chunk + 1) * CHUNK_COLS]
+                )
+                x_raw[(chunk, tt)] = raw
+
+        def load_w(step):
+            branch, chunk = steps[step]
+            for piece in range(PIECES):
+                first = chunk * CHUNK_GROUPS + piece * PIECE_GROUPS
+                w_piece = w_pool.tile([P, PIECE_GROUPS, F], U32, name="w_piece", tag="w_piece", align_bytes=64)
+                nc.sync.dma_start(
+                    out=w_piece[:].bitcast(I32),
+                    in_=words_of[branch][first : first + PIECE_GROUPS]
+                    .rearrange("g p n t -> p g (n t)")
+                    .bitcast(I32),
+                )
+                w_pieces[(step, piece)] = w_piece
+
+        def prepare_x(chunk):
+            grouped_tiles = []
+            for tt in range(TOKEN_TILES):
+                words = x_raw[(chunk, tt)][:].bitcast(F32)
+                grouped = grouped_pool.tile(
+                    [P, CHUNK_GROUPS, P, PACK], BF16, name="grouped", tag="grouped", align_bytes=64
+                )
+                grouped_words = grouped[:].bitcast(F32)
+                for bank in range(CHUNK_GROUPS // BANK_GROUPS):
+                    turned = turn_psum.tile([P, BANK_GROUPS, 2, P], F32, name="turned", tag="turn")
+                    for i in range(BANK_GROUPS):
+                        first = (bank * BANK_GROUPS + i) * WORDS_PER_GROUP
+                        for u in range(2):
+                            nc.tensor.transpose(
+                                turned[:, i, u, :],
+                                words[:, first + u : first + WORDS_PER_GROUP : 2],
+                                identity_f32[:],
+                            )
+                    copy_out = nc.scalar.copy if bank % 2 == 0 else nc.vector.tensor_copy
+                    copy_out(
+                        out=grouped_words[:, bank * BANK_GROUPS : (bank + 1) * BANK_GROUPS, :, :],
+                        in_=turned[:].rearrange("p g u t -> p g t u"),
+                    )
+                grouped_tiles.append(grouped)
+            for tt in range(TOKEN_TILES):
+                codes = keep.tile(
+                    [P, CHUNK_GROUPS, P], U32, name="x_codes_%d_%d" % (chunk, tt), align_bytes=64
+                )
+                scales = keep.tile(
+                    [P, CHUNK_GROUPS, P], U8, name="x_scales_%d_%d" % (chunk, tt), align_bytes=64
+                )
+                nc.vector.quantize_mx(
+                    out=codes[:].rearrange("p g t -> p (g t)").bitcast(FP8X4),
+                    scales=scales[:].rearrange("p g t -> p (g t)"),
+                    in_=grouped_tiles[tt][:].rearrange("p g t j -> p (g t j)"),
+                )
+                x_codes[(chunk, tt)] = codes
+                x_scales[(chunk, tt)] = scales
+
+        def multiply(step, acc):
+            branch, chunk = steps[step]
+            for piece in range(PIECES):
+                for i in range(PIECE_GROUPS):
+                    local = piece * PIECE_GROUPS + i
+                    for tt in range(TOKEN_TILES):
+                        nc.tensor.matmul_mx(
+                            out=acc[(branch, tt)][:],
+                            lhsT=x_codes[(chunk, tt)][:, local, :].bitcast(FP8X4),
+                            lhsT_scale=x_scales[(chunk, tt)][:, local, :],
+                            rhs=w_pieces[(step, piece)][:, i, :].bitcast(FP8X4),
+                            rhs_scale=planes[(branch, chunk)][4 * chunk : P, local, :],
+                            start=(chunk == 0 and local == 0),
+                            stop=(chunk == CHUNKS - 1 and local == CHUNK_GROUPS - 1),
+                        )
+
+        lora_in = {}
+        for branch in branches:
+            xa, lora_b = lora_inputs[branch]
+            lora_in[branch] = keep.tile([P, TOKEN_TILES + F // P, R], BF16, name="lora_in_" + branch)
+            nc.scalar.dma_start(
+                out=lora_in[branch][:, 0:TOKEN_TILES, :], in_=xa.rearrange("b s r -> s b r")
+            )
+            nc.scalar.dma_start(
+                out=lora_in[branch][:, TOKEN_TILES:, :],
+                in_=lora_b.rearrange("(j p) r -> p j r", p=P),
+            )
+        load_x(0)
+        load_x(1)
+        load_w(0)
+
+        lora_turned = {}
+        for branch in branches:
+            turned = turn_psum.tile([P, TOKEN_TILES + F // P, P], BF16, name="lora_ps", tag="turn")
+            for i in range(TOKEN_TILES + F // P):
+                nc.tensor.transpose(turned[:, i, :], lora_in[branch][:, i, :], identity_bf16[:])
+            lora_turned[branch] = keep.tile(
+                [P, TOKEN_TILES + F // P, P], BF16, name="lora_turned_" + branch
+            )
+            nc.scalar.copy(out=lora_turned[branch][:], in_=turned[:])
+
+        prepare_x(0)
+
+        lora_term = {}
+        for branch in branches:
+            for tt in range(TOKEN_TILES):
+                product = acc_psum.tile([P, F], F32, name="product", tag="acc_%s_%d" % (branch, tt))
+                nc.tensor.matmul(
+                    out=product[:],
+                    lhsT=lora_turned[branch][:, tt, :],
+                    rhs=lora_turned[branch][:, TOKEN_TILES:, :].rearrange("r j p -> r (j p)"),
+                    start=True,
+                    stop=True,
+                )
+                lora_term[(branch, tt)] = keep.tile(
+                    [P, F], F32, name="lora_term_%s_%d" % (branch, tt)
+                )
+                nc.scalar.mul(out=lora_term[(branch, tt)][:], in_=product[:], mul=LORA_SCALING)
+
+        acc = {}
+        for branch in branches:
+            for tt in range(TOKEN_TILES):
+                acc[(branch, tt)] = acc_psum.tile(
+                    [P, F], F32, name="acc_%s_%d" % (branch, tt), tag="acc_%s_%d" % (branch, tt)
+                )
+
+        gate = {}
+        for step in range(len(steps)):
+            if step + 2 < CHUNKS:
+                load_x(step + 2)
+            if step + 1 < len(steps):
+                load_w(step + 1)
+            if step + 1 < CHUNKS:
+                prepare_x(step + 1)
+            multiply(step, acc)
+            if step == CHUNKS - 1:
+                for tt in range(TOKEN_TILES):
+                    h1 = keep.tile([P, F], F32, name="h1_%d" % tt)
+                    nc.vector.tensor_add(
+                        out=h1[:], in0=acc[("w1", tt)][:], in1=lora_term[("w1", tt)][:]
+                    )
+                    gate[tt] = keep.tile([P, F], F32, name="gate_%d" % tt)
+                    nc.scalar.activation(out=gate[tt][:], in_=h1[:], func=SILU)
+
+        h3 = {}
+        g_sorted = {}
+        for tt in range(TOKEN_TILES):
+            h3[tt] = keep.tile([P, F], F32, name="h3_%d" % tt)
+            nc.vector.tensor_add(out=h3[tt][:], in0=acc[("w3", tt)][:], in1=lora_term[("w3", tt)][:])
+            g_sorted[tt] = keep.tile([P, PACK, P], BF16, name="g_sorted_%d" % tt)
+            nc.vector.tensor_mul(
+                out=g_sorted[tt][:],
+                in0=h3[tt][:].rearrange("s (p t) -> s t p", t=PACK),
+                in1=gate[tt][:].rearrange("s (p t) -> s t p", t=PACK),
+            )
+        g_grouped = keep.tile([P, TOKEN_TILES, P, PACK], BF16, name="g_grouped", align_bytes=64)
+        for tt in range(TOKEN_TILES):
+            g_turned = turn_psum.tile([P, PACK, P], BF16, name="g_turned", tag="turn")
+            for t in range(PACK):
+                nc.tensor.transpose(g_turned[:, t, :], g_sorted[tt][:, t, :], identity_bf16[:])
+            nc.scalar.copy(out=g_grouped[:, tt, :, :], in_=g_turned[:].rearrange("p t s -> p s t"))
+        for tt in range(TOKEN_TILES):
+            g = keep.tile([P, F], F32, name="g_%d" % tt)
+            nc.vector.tensor_mul(out=g[:], in0=h3[tt][:], in1=gate[tt][:])
+            nc.sync.dma_start(out=out_0[tt], in_=g[:])
+        g_codes = keep.tile([P, TOKEN_TILES, P], U32, name="g_codes", align_bytes=64)
+        g_scales = keep.tile([P, TOKEN_TILES, P], U8, name="g_scales", align_bytes=64)
+        nc.vector.quantize_mx(
+            out=g_codes[:].rearrange("p b s -> p (b s)").bitcast(FP8X4),
+            scales=g_scales[:].rearrange("p b s -> p (b s)"),
+            in_=g_grouped[:].rearrange("p b s t -> p (b s t)"),
+        )
+        ga2_psum = turn_psum.tile([P, TOKEN_TILES, R], F32, name="ga2_psum", tag="turn")
+        for tt in range(TOKEN_TILES):
+            nc.tensor.matmul_mx(
+                out=ga2_psum[:, tt, :],
+                lhsT=g_codes[:, tt, :].bitcast(FP8X4),
+                lhsT_scale=g_scales[:, tt, :],
+                rhs=a2_words[:].bitcast(FP8X4),
+                rhs_scale=a2_plane[:],
+                start=True,
+                stop=True,
+            )
+        ga2 = keep.tile([P, TOKEN_TILES, R], F32, name="ga2")
+        nc.scalar.copy(out=ga2[:], in_=ga2_psum[:])
+        nc.sync.dma_start(out=out_1.rearrange("b s r -> s b r"), in_=ga2[:])

@@ -24,7 +24,8 @@ CHUNK_COLS = K_PASS * CHUNK_GROUPS
 PIECE_GROUPS = 2
 PIECES = CHUNK_GROUPS // PIECE_GROUPS
 BANK_GROUPS = 2
-WORDS_PER_GROUP = K_PASS // 2
+SCALES_AHEAD = 3
+LORA_STEP = 1
 LORA_SCALING = 2.0
 
 FLOPS = 2 * TOKEN_TILES * P * (2 * D * F + 2 * R * F + F * R)
@@ -56,6 +57,7 @@ def tile_feedforward_pa_k_kernel(
     with ExitStack() as ctx:
         keep = ctx.enter_context(tc.tile_pool(name="keep", bufs=1))
         x_pool = ctx.enter_context(tc.tile_pool(name="x_pool", bufs=2 * TOKEN_TILES))
+        sorted_pool = ctx.enter_context(tc.tile_pool(name="sorted_pool", bufs=TOKEN_TILES))
         grouped_pool = ctx.enter_context(tc.tile_pool(name="grouped_pool", bufs=TOKEN_TILES))
         w_pool = ctx.enter_context(tc.tile_pool(name="w_pool", bufs=3 * PIECES))
         turn_psum = ctx.enter_context(tc.psum_pool(name="turn_psum", bufs=4))
@@ -63,11 +65,23 @@ def tile_feedforward_pa_k_kernel(
         ctx.enter_context(tc.manual_schedule())
 
         planes = {}
-        for branch, chunk in steps:
-            planes[(branch, chunk)] = keep.tile(
+
+        def load_scales(step):
+            branch, chunk = steps[step]
+            plane = keep.tile(
                 [P, CHUNK_GROUPS, F], U8, name="planes_%s_%d" % (branch, chunk), align_bytes=64
             )
-            nc.vector.memset(planes[(branch, chunk)][:].bitcast(I32), 0)
+            nc.vector.memset(plane[:].bitcast(I32), 0)
+            rows = scales_of[branch].bitcast(F32)[
+                chunk * CHUNK_GROUPS : (chunk + 1) * CHUNK_GROUPS
+            ]
+            for r in range(4):
+                nc.gpsimd.dma_start(
+                    out=plane[4 * chunk + r : P : 32, :, :].bitcast(F32),
+                    in_=rows[:, r : 16 : 4, :].rearrange("g q n -> q g n"),
+                )
+            planes[(branch, chunk)] = plane
+
         a2_plane = keep.tile([P, R], U8, name="a2_plane", align_bytes=64)
         nc.vector.memset(a2_plane[:].bitcast(I32), 0)
 
@@ -76,15 +90,8 @@ def tile_feedforward_pa_k_kernel(
         identity_bf16 = keep.tile([P, P], BF16, name="identity_bf16")
         make_identity(nc, identity_bf16[:])
 
-        for branch, chunk in steps:
-            rows = scales_of[branch].bitcast(F32)[
-                chunk * CHUNK_GROUPS : (chunk + 1) * CHUNK_GROUPS
-            ]
-            for r in range(4):
-                nc.gpsimd.dma_start(
-                    out=planes[(branch, chunk)][4 * chunk + r : P : 32, :, :].bitcast(F32),
-                    in_=rows[:, r : 16 : 4, :].rearrange("g q n -> q g n"),
-                )
+        for step in range(SCALES_AHEAD):
+            load_scales(step)
         a2_words = keep.tile([P, R], U32, name="a2_words", align_bytes=64)
         nc.gpsimd.dma_start(
             out=a2_words[:].bitcast(F32),
@@ -123,9 +130,20 @@ def tile_feedforward_pa_k_kernel(
                 w_pieces[(step, piece)] = w_piece
 
         def prepare_x(chunk):
+            sorted_tiles = []
+            for tt in range(TOKEN_TILES):
+                sorted_words = sorted_pool.tile(
+                    [P, CHUNK_GROUPS, 2, P], F32, name="sorted_words", tag="sorted_words"
+                )
+                nc.vector.tensor_copy(
+                    out=sorted_words[:],
+                    in_=x_raw[(chunk, tt)][:]
+                    .bitcast(F32)
+                    .rearrange("s (g p u) -> s g u p", g=CHUNK_GROUPS, u=2),
+                )
+                sorted_tiles.append(sorted_words)
             grouped_tiles = []
             for tt in range(TOKEN_TILES):
-                words = x_raw[(chunk, tt)][:].bitcast(F32)
                 grouped = grouped_pool.tile(
                     [P, CHUNK_GROUPS, P, PACK], BF16, name="grouped", tag="grouped", align_bytes=64
                 )
@@ -133,11 +151,10 @@ def tile_feedforward_pa_k_kernel(
                 for bank in range(CHUNK_GROUPS // BANK_GROUPS):
                     turned = turn_psum.tile([P, BANK_GROUPS, 2, P], F32, name="turned", tag="turn")
                     for i in range(BANK_GROUPS):
-                        first = (bank * BANK_GROUPS + i) * WORDS_PER_GROUP
                         for u in range(2):
                             nc.tensor.transpose(
                                 turned[:, i, u, :],
-                                words[:, first + u : first + WORDS_PER_GROUP : 2],
+                                sorted_tiles[tt][:, bank * BANK_GROUPS + i, u, :],
                                 identity_f32[:],
                             )
                     copy_out = nc.scalar.copy if bank % 2 == 0 else nc.vector.tensor_copy
@@ -178,47 +195,56 @@ def tile_feedforward_pa_k_kernel(
                         )
 
         lora_in = {}
-        for branch in branches:
-            xa, lora_b = lora_inputs[branch]
-            lora_in[branch] = keep.tile([P, TOKEN_TILES + F // P, R], BF16, name="lora_in_" + branch)
-            nc.scalar.dma_start(
-                out=lora_in[branch][:, 0:TOKEN_TILES, :], in_=xa.rearrange("b s r -> s b r")
-            )
-            nc.scalar.dma_start(
-                out=lora_in[branch][:, TOKEN_TILES:, :],
-                in_=lora_b.rearrange("(j p) r -> p j r", p=P),
-            )
+        lora_turned = {}
+        lora_term = {}
+
+        def load_lora():
+            for branch in branches:
+                xa, lora_b = lora_inputs[branch]
+                lora_in[branch] = keep.tile(
+                    [P, TOKEN_TILES + F // P, R], BF16, name="lora_in_" + branch
+                )
+                nc.sync.dma_start(
+                    out=lora_in[branch][:, 0:TOKEN_TILES, :], in_=xa.rearrange("b s r -> s b r")
+                )
+                nc.sync.dma_start(
+                    out=lora_in[branch][:, TOKEN_TILES:, :],
+                    in_=lora_b.rearrange("(j p) r -> p j r", p=P),
+                )
+
+        def transpose_lora():
+            for branch in branches:
+                turned = turn_psum.tile(
+                    [P, TOKEN_TILES + F // P, P], BF16, name="lora_ps", tag="turn"
+                )
+                for i in range(TOKEN_TILES + F // P):
+                    nc.tensor.transpose(turned[:, i, :], lora_in[branch][:, i, :], identity_bf16[:])
+                lora_turned[branch] = keep.tile(
+                    [P, TOKEN_TILES + F // P, P], BF16, name="lora_turned_" + branch
+                )
+                nc.scalar.copy(out=lora_turned[branch][:], in_=turned[:])
+
+        def multiply_lora():
+            for branch in branches:
+                for tt in range(TOKEN_TILES):
+                    product = turn_psum.tile([P, F], F32, name="product", tag="turn")
+                    nc.tensor.matmul(
+                        out=product[:],
+                        lhsT=lora_turned[branch][:, tt, :],
+                        rhs=lora_turned[branch][:, TOKEN_TILES:, :].rearrange("r j p -> r (j p)"),
+                        start=True,
+                        stop=True,
+                    )
+                    lora_term[(branch, tt)] = keep.tile(
+                        [P, F], F32, name="lora_term_%s_%d" % (branch, tt)
+                    )
+                    nc.scalar.mul(out=lora_term[(branch, tt)][:], in_=product[:], mul=LORA_SCALING)
+
         load_x(0)
         load_x(1)
         load_w(0)
-
-        lora_turned = {}
-        for branch in branches:
-            turned = turn_psum.tile([P, TOKEN_TILES + F // P, P], BF16, name="lora_ps", tag="turn")
-            for i in range(TOKEN_TILES + F // P):
-                nc.tensor.transpose(turned[:, i, :], lora_in[branch][:, i, :], identity_bf16[:])
-            lora_turned[branch] = keep.tile(
-                [P, TOKEN_TILES + F // P, P], BF16, name="lora_turned_" + branch
-            )
-            nc.scalar.copy(out=lora_turned[branch][:], in_=turned[:])
-
+        load_lora()
         prepare_x(0)
-
-        lora_term = {}
-        for branch in branches:
-            for tt in range(TOKEN_TILES):
-                product = acc_psum.tile([P, F], F32, name="product", tag="acc_%s_%d" % (branch, tt))
-                nc.tensor.matmul(
-                    out=product[:],
-                    lhsT=lora_turned[branch][:, tt, :],
-                    rhs=lora_turned[branch][:, TOKEN_TILES:, :].rearrange("r j p -> r (j p)"),
-                    start=True,
-                    stop=True,
-                )
-                lora_term[(branch, tt)] = keep.tile(
-                    [P, F], F32, name="lora_term_%s_%d" % (branch, tt)
-                )
-                nc.scalar.mul(out=lora_term[(branch, tt)][:], in_=product[:], mul=LORA_SCALING)
 
         acc = {}
         for branch in branches:
@@ -233,8 +259,14 @@ def tile_feedforward_pa_k_kernel(
                 load_x(step + 2)
             if step + 1 < len(steps):
                 load_w(step + 1)
+            if step + SCALES_AHEAD < len(steps):
+                load_scales(step + SCALES_AHEAD)
+            if step == LORA_STEP:
+                transpose_lora()
             if step + 1 < CHUNKS:
                 prepare_x(step + 1)
+            if step == LORA_STEP:
+                multiply_lora()
             multiply(step, acc)
             if step == CHUNKS - 1:
                 for tt in range(TOKEN_TILES):

@@ -24,7 +24,9 @@ CHUNK_COLS = K_PASS * CHUNK_GROUPS
 PIECE_GROUPS = 2
 PIECES = CHUNK_GROUPS // PIECE_GROUPS
 BANK_GROUPS = 2
-SCALES_AHEAD = 3
+GROUPS = D // K_PASS
+PLANE_GROUPS = 16
+ROWS_PER_LOAD = 2
 LORA_STEP = 1
 LORA_SCALING = 2.0
 
@@ -65,22 +67,32 @@ def tile_feedforward_pa_k_kernel(
         ctx.enter_context(tc.manual_schedule())
 
         planes = {}
-
-        def load_scales(step):
-            branch, chunk = steps[step]
-            plane = keep.tile(
-                [P, CHUNK_GROUPS, F], U8, name="planes_%s_%d" % (branch, chunk), align_bytes=64
-            )
-            nc.vector.memset(plane[:].bitcast(I32), 0)
-            rows = scales_of[branch].bitcast(F32)[
-                chunk * CHUNK_GROUPS : (chunk + 1) * CHUNK_GROUPS
-            ]
-            for r in range(4):
-                nc.gpsimd.dma_start(
-                    out=plane[4 * chunk + r : P : 32, :, :].bitcast(F32),
-                    in_=rows[:, r : 16 : 4, :].rearrange("g q n -> q g n"),
+        plane_offset = {}
+        scale_rows = []
+        for branch in branches:
+            for half in range(GROUPS // PLANE_GROUPS):
+                plane = keep.tile(
+                    [P, PLANE_GROUPS, F], U8, name="planes_%s_%d" % (branch, half), align_bytes=64
                 )
-            planes[(branch, chunk)] = plane
+                nc.vector.memset(plane[:].bitcast(I32), 0)
+                planes[(branch, half)] = plane
+                plane_offset[(branch, half)] = 4 * len(plane_offset)
+                for q in range(16):
+                    scale_rows.append((branch, half, q))
+        rows_issued = [0]
+
+        def load_scale_rows():
+            for i in range(ROWS_PER_LOAD):
+                if rows_issued[0] < len(scale_rows):
+                    branch, half, q = scale_rows[rows_issued[0]]
+                    partition = 32 * (q // 4) + q % 4 + plane_offset[(branch, half)]
+                    nc.sync.dma_start(
+                        out=planes[(branch, half)][partition : partition + 1, :, :].bitcast(I32),
+                        in_=scales_of[branch]
+                        .bitcast(I32)[half * PLANE_GROUPS : (half + 1) * PLANE_GROUPS, q : q + 1, :]
+                        .rearrange("g o n -> o g n"),
+                    )
+                    rows_issued[0] = rows_issued[0] + 1
 
         a2_plane = keep.tile([P, R], U8, name="a2_plane", align_bytes=64)
         nc.vector.memset(a2_plane[:].bitcast(I32), 0)
@@ -90,8 +102,6 @@ def tile_feedforward_pa_k_kernel(
         identity_bf16 = keep.tile([P, P], BF16, name="identity_bf16")
         make_identity(nc, identity_bf16[:])
 
-        for step in range(SCALES_AHEAD):
-            load_scales(step)
         a2_words = keep.tile([P, R], U32, name="a2_words", align_bytes=64)
         nc.gpsimd.dma_start(
             out=a2_words[:].bitcast(F32),
@@ -115,6 +125,7 @@ def tile_feedforward_pa_k_kernel(
                     out=raw[:], in_=x[tt, :, chunk * CHUNK_COLS : (chunk + 1) * CHUNK_COLS]
                 )
                 x_raw[(chunk, tt)] = raw
+                load_scale_rows()
 
         def load_w(step):
             branch, chunk = steps[step]
@@ -128,6 +139,7 @@ def tile_feedforward_pa_k_kernel(
                     .bitcast(I32),
                 )
                 w_pieces[(step, piece)] = w_piece
+                load_scale_rows()
 
         def prepare_x(chunk):
             sorted_tiles = []
@@ -183,13 +195,14 @@ def tile_feedforward_pa_k_kernel(
             for piece in range(PIECES):
                 for i in range(PIECE_GROUPS):
                     local = piece * PIECE_GROUPS + i
+                    half, in_plane = divmod(chunk * CHUNK_GROUPS + local, PLANE_GROUPS)
                     for tt in range(TOKEN_TILES):
                         nc.tensor.matmul_mx(
                             out=acc[(branch, tt)][:],
                             lhsT=x_codes[(chunk, tt)][:, local, :].bitcast(FP8X4),
                             lhsT_scale=x_scales[(chunk, tt)][:, local, :],
                             rhs=w_pieces[(step, piece)][:, i, :].bitcast(FP8X4),
-                            rhs_scale=planes[(branch, chunk)][4 * chunk : P, local, :],
+                            rhs_scale=planes[(branch, half)][plane_offset[(branch, half)] : P, in_plane, :],
                             start=(chunk == 0 and local == 0),
                             stop=(chunk == CHUNKS - 1 and local == CHUNK_GROUPS - 1),
                         )
@@ -259,8 +272,6 @@ def tile_feedforward_pa_k_kernel(
                 load_x(step + 2)
             if step + 1 < len(steps):
                 load_w(step + 1)
-            if step + SCALES_AHEAD < len(steps):
-                load_scales(step + SCALES_AHEAD)
             if step == LORA_STEP:
                 transpose_lora()
             if step + 1 < CHUNKS:

@@ -18,16 +18,16 @@ F = 512
 R = 128
 PACK = 4
 K_PASS = P * PACK
-CHUNK_GROUPS = 8
-CHUNKS = D // (K_PASS * CHUNK_GROUPS)
-CHUNK_COLS = K_PASS * CHUNK_GROUPS
-PIECE_GROUPS = 2
-PIECES = CHUNK_GROUPS // PIECE_GROUPS
-BANK_GROUPS = 2
 GROUPS = D // K_PASS
-PLANE_GROUPS = 16
-ROWS_PER_LOAD = 2
-LORA_STEP = 1
+ROUND_GROUPS = 4
+ROUNDS = GROUPS // ROUND_GROUPS
+ROUND_COLS = K_PASS * ROUND_GROUPS
+PIECE_GROUPS = 2
+PIECES = ROUND_GROUPS // PIECE_GROUPS
+BANK_GROUPS = 2
+PLANE_GROUPS = 8
+LORA_ROUND = 1
+LORA_BLOCKS = TOKEN_TILES + F // P
 LORA_SCALING = 2.0
 
 FLOPS = 2 * TOKEN_TILES * P * (2 * D * F + 2 * R * F + F * R)
@@ -54,113 +54,101 @@ def tile_feedforward_pa_k_kernel(
     words_of = {"w1": w1_words, "w3": w3_words}
     scales_of = {"w1": w1_scales, "w3": w3_scales}
     lora_inputs = {"w1": (xa1, lora_B1), "w3": (xa3, lora_B3)}
-    steps = [(branch, chunk) for branch in branches for chunk in range(CHUNKS)]
 
     with ExitStack() as ctx:
         keep = ctx.enter_context(tc.tile_pool(name="keep", bufs=1))
-        x_pool = ctx.enter_context(tc.tile_pool(name="x_pool", bufs=2 * TOKEN_TILES))
-        sorted_pool = ctx.enter_context(tc.tile_pool(name="sorted_pool", bufs=TOKEN_TILES))
-        grouped_pool = ctx.enter_context(tc.tile_pool(name="grouped_pool", bufs=TOKEN_TILES))
-        w_pool = ctx.enter_context(tc.tile_pool(name="w_pool", bufs=3 * PIECES))
+        x_pool = ctx.enter_context(tc.tile_pool(name="x_pool", bufs=3 * TOKEN_TILES))
+        sorted_pool = ctx.enter_context(tc.tile_pool(name="sorted_pool", bufs=2 * TOKEN_TILES))
+        grouped_pool = ctx.enter_context(tc.tile_pool(name="grouped_pool", bufs=2))
+        codes_pool = ctx.enter_context(tc.tile_pool(name="codes_pool", bufs=3))
+        w_pool = ctx.enter_context(tc.tile_pool(name="w_pool", bufs=4 * 2 * PIECES))
         turn_psum = ctx.enter_context(tc.psum_pool(name="turn_psum", bufs=4))
         acc_psum = ctx.enter_context(tc.psum_pool(name="acc_psum", bufs=1))
         ctx.enter_context(tc.manual_schedule())
-
-        planes = {}
-        plane_offset = {}
-        scale_rows = []
-        for branch in branches:
-            for half in range(GROUPS // PLANE_GROUPS):
-                plane = keep.tile(
-                    [P, PLANE_GROUPS, F], U8, name="planes_%s_%d" % (branch, half), align_bytes=64
-                )
-                nc.vector.memset(plane[:].bitcast(I32), 0)
-                planes[(branch, half)] = plane
-                plane_offset[(branch, half)] = 4 * len(plane_offset)
-                for q in range(16):
-                    scale_rows.append((branch, half, q))
-        rows_issued = [0]
-
-        def load_scale_rows():
-            for i in range(ROWS_PER_LOAD):
-                if rows_issued[0] < len(scale_rows):
-                    branch, half, q = scale_rows[rows_issued[0]]
-                    partition = 32 * (q // 4) + q % 4 + plane_offset[(branch, half)]
-                    nc.sync.dma_start(
-                        out=planes[(branch, half)][partition : partition + 1, :, :].bitcast(I32),
-                        in_=scales_of[branch]
-                        .bitcast(I32)[half * PLANE_GROUPS : (half + 1) * PLANE_GROUPS, q : q + 1, :]
-                        .rearrange("g o n -> o g n"),
-                    )
-                    rows_issued[0] = rows_issued[0] + 1
-
-        a2_plane = keep.tile([P, R], U8, name="a2_plane", align_bytes=64)
-        nc.vector.memset(a2_plane[:].bitcast(I32), 0)
-
-        identity_f32 = keep.tile([P, P], F32, name="identity_f32")
-        make_identity(nc, identity_f32[:])
-        identity_bf16 = keep.tile([P, P], BF16, name="identity_bf16")
-        make_identity(nc, identity_bf16[:])
-
-        a2_words = keep.tile([P, R], U32, name="a2_words", align_bytes=64)
-        nc.gpsimd.dma_start(
-            out=a2_words[:].bitcast(F32),
-            in_=lora_A2_words[0].rearrange("p n t -> p (n t)").bitcast(F32),
-        )
-        for r in range(4):
-            nc.gpsimd.dma_start(
-                out=a2_plane[r : P : 32, :].bitcast(F32),
-                in_=lora_A2_scales[0].bitcast(F32)[r : 16 : 4, :],
-            )
 
         x_raw = {}
         x_codes = {}
         x_scales = {}
         w_pieces = {}
+        planes = {}
+        lora_in = {}
+        lora_turned = {}
+        lora_term = {}
+        acc = {}
+        gate = {}
 
-        def load_x(chunk):
-            for tt in range(TOKEN_TILES):
-                raw = x_pool.tile([P, CHUNK_COLS], BF16, name="x_raw", tag="x_raw")
-                nc.sync.dma_start(
-                    out=raw[:], in_=x[tt, :, chunk * CHUNK_COLS : (chunk + 1) * CHUNK_COLS]
+        def load_x(rnd, tt):
+            raw = x_pool.tile([P, ROUND_COLS], BF16, name="x_raw", tag="x_raw")
+            nc.sync.dma_start(out=raw[:], in_=x[tt, :, rnd * ROUND_COLS : (rnd + 1) * ROUND_COLS])
+            x_raw[(rnd, tt)] = raw
+
+        def load_w(rnd):
+            for branch in branches:
+                for piece in range(PIECES):
+                    first = rnd * ROUND_GROUPS + piece * PIECE_GROUPS
+                    w_piece = w_pool.tile(
+                        [P, PIECE_GROUPS, F], U32, name="w_piece", tag="w_piece", align_bytes=64
+                    )
+                    nc.sync.dma_start(
+                        out=w_piece[:].bitcast(I32),
+                        in_=words_of[branch][first : first + PIECE_GROUPS]
+                        .rearrange("g p n t -> p g (n t)")
+                        .bitcast(I32),
+                    )
+                    w_pieces[(rnd, branch, piece)] = w_piece
+
+        def load_scale_rows(queue, view, branch, chunk, rows):
+            source = scales_of[branch].bitcast(view)[
+                chunk * PLANE_GROUPS : (chunk + 1) * PLANE_GROUPS
+            ]
+            for r in rows:
+                queue.dma_start(
+                    out=planes[(branch, chunk)][4 * chunk + r : P : 32, :, :].bitcast(view),
+                    in_=source[:, r : 16 : 4, :].rearrange("g q n -> q g n"),
                 )
-                x_raw[(chunk, tt)] = raw
-                load_scale_rows()
 
-        def load_w(step):
-            branch, chunk = steps[step]
-            for piece in range(PIECES):
-                first = chunk * CHUNK_GROUPS + piece * PIECE_GROUPS
-                w_piece = w_pool.tile([P, PIECE_GROUPS, F], U32, name="w_piece", tag="w_piece", align_bytes=64)
-                nc.sync.dma_start(
-                    out=w_piece[:].bitcast(I32),
-                    in_=words_of[branch][first : first + PIECE_GROUPS]
-                    .rearrange("g p n t -> p g (n t)")
-                    .bitcast(I32),
+        def zero_planes(chunk):
+            for branch in branches:
+                planes[(branch, chunk)] = keep.tile(
+                    [P, PLANE_GROUPS, F], U8, name="planes_%s_%d" % (branch, chunk), align_bytes=64
                 )
-                w_pieces[(step, piece)] = w_piece
-                load_scale_rows()
+                nc.vector.memset(planes[(branch, chunk)][:].bitcast(I32), 0)
 
-        def prepare_x(chunk):
+        def load_lora():
+            for branch in branches:
+                xa, lora_b = lora_inputs[branch]
+                lora_in[branch] = keep.tile([P, LORA_BLOCKS, R], BF16, name="lora_in_" + branch)
+                nc.sync.dma_start(
+                    out=lora_in[branch][:, 0:TOKEN_TILES, :], in_=xa.rearrange("b s r -> s b r")
+                )
+                nc.sync.dma_start(
+                    out=lora_in[branch][:, TOKEN_TILES:, :],
+                    in_=lora_b.rearrange("(j p) r -> p j r", p=P),
+                )
+
+        def prepare_x(rnd):
             sorted_tiles = []
             for tt in range(TOKEN_TILES):
                 sorted_words = sorted_pool.tile(
-                    [P, CHUNK_GROUPS, 2, P], F32, name="sorted_words", tag="sorted_words"
+                    [P, ROUND_GROUPS, 2, P], F32, name="sorted_words", tag="sorted_words"
                 )
                 nc.vector.tensor_copy(
                     out=sorted_words[:],
-                    in_=x_raw[(chunk, tt)][:]
+                    in_=x_raw[(rnd, tt)][:]
                     .bitcast(F32)
-                    .rearrange("s (g p u) -> s g u p", g=CHUNK_GROUPS, u=2),
+                    .rearrange("s (g p u) -> s g u p", g=ROUND_GROUPS, u=2),
                 )
                 sorted_tiles.append(sorted_words)
-            grouped_tiles = []
+            grouped = grouped_pool.tile(
+                [P, TOKEN_TILES, ROUND_GROUPS, P, PACK],
+                BF16,
+                name="grouped",
+                tag="grouped",
+                align_bytes=64,
+            )
+            grouped_words = grouped[:].bitcast(F32)
             for tt in range(TOKEN_TILES):
-                grouped = grouped_pool.tile(
-                    [P, CHUNK_GROUPS, P, PACK], BF16, name="grouped", tag="grouped", align_bytes=64
-                )
-                grouped_words = grouped[:].bitcast(F32)
-                for bank in range(CHUNK_GROUPS // BANK_GROUPS):
+                for bank in range(ROUND_GROUPS // BANK_GROUPS):
                     turned = turn_psum.tile([P, BANK_GROUPS, 2, P], F32, name="turned", tag="turn")
                     for i in range(BANK_GROUPS):
                         for u in range(2):
@@ -171,69 +159,49 @@ def tile_feedforward_pa_k_kernel(
                             )
                     copy_out = nc.scalar.copy if bank % 2 == 0 else nc.vector.tensor_copy
                     copy_out(
-                        out=grouped_words[:, bank * BANK_GROUPS : (bank + 1) * BANK_GROUPS, :, :],
+                        out=grouped_words[
+                            :, tt, bank * BANK_GROUPS : (bank + 1) * BANK_GROUPS, :, :
+                        ],
                         in_=turned[:].rearrange("p g u t -> p g t u"),
                     )
-                grouped_tiles.append(grouped)
-            for tt in range(TOKEN_TILES):
-                codes = keep.tile(
-                    [P, CHUNK_GROUPS, P], U32, name="x_codes_%d_%d" % (chunk, tt), align_bytes=64
-                )
-                scales = keep.tile(
-                    [P, CHUNK_GROUPS, P], U8, name="x_scales_%d_%d" % (chunk, tt), align_bytes=64
-                )
-                nc.vector.quantize_mx(
-                    out=codes[:].rearrange("p g t -> p (g t)").bitcast(FP8X4),
-                    scales=scales[:].rearrange("p g t -> p (g t)"),
-                    in_=grouped_tiles[tt][:].rearrange("p g t j -> p (g t j)"),
-                )
-                x_codes[(chunk, tt)] = codes
-                x_scales[(chunk, tt)] = scales
+            codes = codes_pool.tile(
+                [P, TOKEN_TILES, ROUND_GROUPS, P], U32, name="x_codes", tag="x_codes", align_bytes=64
+            )
+            scales = codes_pool.tile(
+                [P, TOKEN_TILES, ROUND_GROUPS, P], U8, name="x_scales", tag="x_scales", align_bytes=64
+            )
+            nc.vector.quantize_mx(
+                out=codes[:].rearrange("p b g t -> p (b g t)").bitcast(FP8X4),
+                scales=scales[:].rearrange("p b g t -> p (b g t)"),
+                in_=grouped[:].rearrange("p b g t j -> p (b g t j)"),
+            )
+            x_codes[rnd] = codes
+            x_scales[rnd] = scales
 
-        def multiply(step, acc):
-            branch, chunk = steps[step]
+        def multiply(rnd, branch):
             for piece in range(PIECES):
-                for i in range(PIECE_GROUPS):
-                    local = piece * PIECE_GROUPS + i
-                    half, in_plane = divmod(chunk * CHUNK_GROUPS + local, PLANE_GROUPS)
-                    for tt in range(TOKEN_TILES):
+                for tt in range(TOKEN_TILES):
+                    for i in range(PIECE_GROUPS):
+                        local = piece * PIECE_GROUPS + i
+                        group = rnd * ROUND_GROUPS + local
+                        chunk, in_plane = divmod(group, PLANE_GROUPS)
                         nc.tensor.matmul_mx(
                             out=acc[(branch, tt)][:],
-                            lhsT=x_codes[(chunk, tt)][:, local, :].bitcast(FP8X4),
-                            lhsT_scale=x_scales[(chunk, tt)][:, local, :],
-                            rhs=w_pieces[(step, piece)][:, i, :].bitcast(FP8X4),
-                            rhs_scale=planes[(branch, half)][plane_offset[(branch, half)] : P, in_plane, :],
-                            start=(chunk == 0 and local == 0),
-                            stop=(chunk == CHUNKS - 1 and local == CHUNK_GROUPS - 1),
+                            lhsT=x_codes[rnd][:, tt, local, :].bitcast(FP8X4),
+                            lhsT_scale=x_scales[rnd][:, tt, local, :],
+                            rhs=w_pieces[(rnd, branch, piece)][:, i, :].bitcast(FP8X4),
+                            rhs_scale=planes[(branch, chunk)][4 * chunk : P, in_plane, :],
+                            start=(group == 0),
+                            stop=(group == GROUPS - 1),
                         )
-
-        lora_in = {}
-        lora_turned = {}
-        lora_term = {}
-
-        def load_lora():
-            for branch in branches:
-                xa, lora_b = lora_inputs[branch]
-                lora_in[branch] = keep.tile(
-                    [P, TOKEN_TILES + F // P, R], BF16, name="lora_in_" + branch
-                )
-                nc.sync.dma_start(
-                    out=lora_in[branch][:, 0:TOKEN_TILES, :], in_=xa.rearrange("b s r -> s b r")
-                )
-                nc.sync.dma_start(
-                    out=lora_in[branch][:, TOKEN_TILES:, :],
-                    in_=lora_b.rearrange("(j p) r -> p j r", p=P),
-                )
 
         def transpose_lora():
             for branch in branches:
-                turned = turn_psum.tile(
-                    [P, TOKEN_TILES + F // P, P], BF16, name="lora_ps", tag="turn"
-                )
-                for i in range(TOKEN_TILES + F // P):
+                turned = turn_psum.tile([P, LORA_BLOCKS, P], BF16, name="lora_ps", tag="turn")
+                for i in range(LORA_BLOCKS):
                     nc.tensor.transpose(turned[:, i, :], lora_in[branch][:, i, :], identity_bf16[:])
                 lora_turned[branch] = keep.tile(
-                    [P, TOKEN_TILES + F // P, P], BF16, name="lora_turned_" + branch
+                    [P, LORA_BLOCKS, P], BF16, name="lora_turned_" + branch
                 )
                 nc.scalar.copy(out=lora_turned[branch][:], in_=turned[:])
 
@@ -253,33 +221,62 @@ def tile_feedforward_pa_k_kernel(
                     )
                     nc.scalar.mul(out=lora_term[(branch, tt)][:], in_=product[:], mul=LORA_SCALING)
 
-        load_x(0)
-        load_x(1)
+        identity_f32 = keep.tile([P, P], F32, name="identity_f32")
+        make_identity(nc, identity_f32[:])
+        identity_bf16 = keep.tile([P, P], BF16, name="identity_bf16")
+        make_identity(nc, identity_bf16[:])
+        table_in = keep.tile([P, 1], F32, name="table_in")
+        table_out = keep.tile([P, 1], F32, name="table_out")
+        nc.vector.memset(table_in[:], 0.0)
+        nc.scalar.activation(out=table_out[:], in_=table_in[:], func=SILU)
+        for branch in branches:
+            for tt in range(TOKEN_TILES):
+                acc[(branch, tt)] = acc_psum.tile([P, F], F32, name="acc_%s_%d" % (branch, tt))
+
+        zero_planes(0)
+        for rnd in range(2):
+            for tt in range(TOKEN_TILES):
+                load_x(rnd, tt)
+                load_scale_rows(nc.sync, I32, branches[rnd], 0, (2 * tt, 2 * tt + 1))
+        zero_planes(1)
+        for branch in branches:
+            load_scale_rows(nc.gpsimd, F32, branch, 1, range(4))
         load_w(0)
         load_lora()
         prepare_x(0)
 
-        acc = {}
-        for branch in branches:
-            for tt in range(TOKEN_TILES):
-                acc[(branch, tt)] = acc_psum.tile(
-                    [P, F], F32, name="acc_%s_%d" % (branch, tt), tag="acc_%s_%d" % (branch, tt)
-                )
+        a2_words = keep.tile([P, R], U32, name="a2_words", align_bytes=64)
+        a2_plane = keep.tile([P, R], U8, name="a2_plane", align_bytes=64)
 
-        gate = {}
-        for step in range(len(steps)):
-            if step + 2 < CHUNKS:
-                load_x(step + 2)
-            if step + 1 < len(steps):
-                load_w(step + 1)
-            if step == LORA_STEP:
+        for rnd in range(ROUNDS):
+            if rnd + 2 < ROUNDS:
+                for tt in range(TOKEN_TILES):
+                    load_x(rnd + 2, tt)
+            if rnd + 1 < ROUNDS:
+                load_w(rnd + 1)
+            if rnd == LORA_ROUND:
                 transpose_lora()
-            if step + 1 < CHUNKS:
-                prepare_x(step + 1)
-            if step == LORA_STEP:
+            if rnd + 1 < ROUNDS:
+                prepare_x(rnd + 1)
+            if rnd == 0:
+                for chunk in range(2, GROUPS // PLANE_GROUPS):
+                    zero_planes(chunk)
+                    for branch in branches:
+                        load_scale_rows(nc.gpsimd, F32, branch, chunk, range(4))
+                nc.vector.memset(a2_plane[:].bitcast(I32), 0)
+                nc.gpsimd.dma_start(
+                    out=a2_words[:].bitcast(F32),
+                    in_=lora_A2_words[0].rearrange("p n t -> p (n t)").bitcast(F32),
+                )
+                for r in range(4):
+                    nc.gpsimd.dma_start(
+                        out=a2_plane[r : P : 32, :].bitcast(F32),
+                        in_=lora_A2_scales[0].bitcast(F32)[r : 16 : 4, :],
+                    )
+            if rnd == LORA_ROUND:
                 multiply_lora()
-            multiply(step, acc)
-            if step == CHUNKS - 1:
+            multiply(rnd, "w1")
+            if rnd == ROUNDS - 1:
                 for tt in range(TOKEN_TILES):
                     h1 = keep.tile([P, F], F32, name="h1_%d" % tt)
                     nc.vector.tensor_add(
@@ -287,6 +284,7 @@ def tile_feedforward_pa_k_kernel(
                     )
                     gate[tt] = keep.tile([P, F], F32, name="gate_%d" % tt)
                     nc.scalar.activation(out=gate[tt][:], in_=h1[:], func=SILU)
+            multiply(rnd, "w3")
 
         h3 = {}
         g_sorted = {}

@@ -26,7 +26,7 @@ PIECE_GROUPS = 2
 PIECES = ROUND_GROUPS // PIECE_GROUPS
 BANK_GROUPS = 2
 PLANE_GROUPS = 8
-LORA_ROUND = 1
+LORA_STEP = 3
 LORA_BLOCKS = TOKEN_TILES + F // P
 LORA_SCALING = 2.0
 
@@ -57,16 +57,18 @@ def tile_feedforward_pa_k_kernel(
 
     with ExitStack() as ctx:
         keep = ctx.enter_context(tc.tile_pool(name="keep", bufs=1))
-        x_pool = ctx.enter_context(tc.tile_pool(name="x_pool", bufs=3 * TOKEN_TILES))
-        sorted_pool = ctx.enter_context(tc.tile_pool(name="sorted_pool", bufs=2 * TOKEN_TILES))
-        grouped_pool = ctx.enter_context(tc.tile_pool(name="grouped_pool", bufs=2))
-        codes_pool = ctx.enter_context(tc.tile_pool(name="codes_pool", bufs=3))
+        x_pool = ctx.enter_context(tc.tile_pool(name="x_pool", bufs=4 * TOKEN_TILES))
+        sorted_pool = ctx.enter_context(tc.tile_pool(name="sorted_pool", bufs=3))
+        grouped_pool = ctx.enter_context(tc.tile_pool(name="grouped_pool", bufs=3))
+        codes_pool = ctx.enter_context(tc.tile_pool(name="codes_pool", bufs=6))
         w_pool = ctx.enter_context(tc.tile_pool(name="w_pool", bufs=4 * 2 * PIECES))
         turn_psum = ctx.enter_context(tc.psum_pool(name="turn_psum", bufs=4))
         acc_psum = ctx.enter_context(tc.psum_pool(name="acc_psum", bufs=1))
         ctx.enter_context(tc.manual_schedule())
 
         x_raw = {}
+        x_sorted = {}
+        x_grouped = {}
         x_codes = {}
         x_scales = {}
         w_pieces = {}
@@ -77,25 +79,25 @@ def tile_feedforward_pa_k_kernel(
         acc = {}
         gate = {}
 
-        def load_x(rnd, tt):
+        def load_x(unit):
+            rnd, tt = divmod(unit, TOKEN_TILES)
             raw = x_pool.tile([P, ROUND_COLS], BF16, name="x_raw", tag="x_raw")
             nc.sync.dma_start(out=raw[:], in_=x[tt, :, rnd * ROUND_COLS : (rnd + 1) * ROUND_COLS])
-            x_raw[(rnd, tt)] = raw
+            x_raw[unit] = raw
 
-        def load_w(rnd):
-            for branch in branches:
-                for piece in range(PIECES):
-                    first = rnd * ROUND_GROUPS + piece * PIECE_GROUPS
-                    w_piece = w_pool.tile(
-                        [P, PIECE_GROUPS, F], U32, name="w_piece", tag="w_piece", align_bytes=64
-                    )
-                    nc.sync.dma_start(
-                        out=w_piece[:].bitcast(I32),
-                        in_=words_of[branch][first : first + PIECE_GROUPS]
-                        .rearrange("g p n t -> p g (n t)")
-                        .bitcast(I32),
-                    )
-                    w_pieces[(rnd, branch, piece)] = w_piece
+        def load_w(rnd, branch):
+            for piece in range(PIECES):
+                first = rnd * ROUND_GROUPS + piece * PIECE_GROUPS
+                w_piece = w_pool.tile(
+                    [P, PIECE_GROUPS, F], U32, name="w_piece", tag="w_piece", align_bytes=64
+                )
+                nc.sync.dma_start(
+                    out=w_piece[:].bitcast(I32),
+                    in_=words_of[branch][first : first + PIECE_GROUPS]
+                    .rearrange("g p n t -> p g (n t)")
+                    .bitcast(I32),
+                )
+                w_pieces[(rnd, branch, piece)] = w_piece
 
         def load_scale_rows(queue, view, branch, chunk, rows):
             source = scales_of[branch].bitcast(view)[
@@ -123,60 +125,53 @@ def tile_feedforward_pa_k_kernel(
                 )
                 nc.sync.dma_start(
                     out=lora_in[branch][:, TOKEN_TILES:, :],
-                    in_=lora_b.rearrange("(j p) r -> p j r", p=P),
+                    in_=lora_b.rearrange("(p t) r -> p t r", t=PACK),
                 )
 
-        def prepare_x(rnd):
-            sorted_tiles = []
-            for tt in range(TOKEN_TILES):
-                sorted_words = sorted_pool.tile(
-                    [P, ROUND_GROUPS, 2, P], F32, name="sorted_words", tag="sorted_words"
-                )
-                nc.vector.tensor_copy(
-                    out=sorted_words[:],
-                    in_=x_raw[(rnd, tt)][:]
-                    .bitcast(F32)
-                    .rearrange("s (g p u) -> s g u p", g=ROUND_GROUPS, u=2),
-                )
-                sorted_tiles.append(sorted_words)
+        def sort_x(unit):
+            x_sorted[unit] = sorted_pool.tile(
+                [P, ROUND_GROUPS, 2, P], F32, name="sorted_words", tag="sorted_words"
+            )
+            nc.vector.tensor_copy(
+                out=x_sorted[unit][:],
+                in_=x_raw[unit][:].bitcast(F32).rearrange("s (g p u) -> s g u p", g=ROUND_GROUPS, u=2),
+            )
+
+        def turn_x(unit):
             grouped = grouped_pool.tile(
-                [P, TOKEN_TILES, ROUND_GROUPS, P, PACK],
-                BF16,
-                name="grouped",
-                tag="grouped",
-                align_bytes=64,
+                [P, ROUND_GROUPS, P, PACK], BF16, name="grouped", tag="grouped", align_bytes=64
             )
             grouped_words = grouped[:].bitcast(F32)
-            for tt in range(TOKEN_TILES):
-                for bank in range(ROUND_GROUPS // BANK_GROUPS):
-                    turned = turn_psum.tile([P, BANK_GROUPS, 2, P], F32, name="turned", tag="turn")
-                    for i in range(BANK_GROUPS):
-                        for u in range(2):
-                            nc.tensor.transpose(
-                                turned[:, i, u, :],
-                                sorted_tiles[tt][:, bank * BANK_GROUPS + i, u, :],
-                                identity_f32[:],
-                            )
-                    copy_out = nc.scalar.copy if bank % 2 == 0 else nc.vector.tensor_copy
-                    copy_out(
-                        out=grouped_words[
-                            :, tt, bank * BANK_GROUPS : (bank + 1) * BANK_GROUPS, :, :
-                        ],
-                        in_=turned[:].rearrange("p g u t -> p g t u"),
-                    )
+            for bank in range(ROUND_GROUPS // BANK_GROUPS):
+                turned = turn_psum.tile([P, BANK_GROUPS, 2, P], F32, name="turned", tag="turn")
+                for i in range(BANK_GROUPS):
+                    for u in range(2):
+                        nc.tensor.transpose(
+                            turned[:, i, u, :],
+                            x_sorted[unit][:, bank * BANK_GROUPS + i, u, :],
+                            identity_f32[:],
+                        )
+                copy_out = nc.scalar.copy if bank % 2 == 0 else nc.vector.tensor_copy
+                copy_out(
+                    out=grouped_words[:, bank * BANK_GROUPS : (bank + 1) * BANK_GROUPS, :, :],
+                    in_=turned[:].rearrange("p g u t -> p g t u"),
+                )
+            x_grouped[unit] = grouped
+
+        def quantise_x(unit):
             codes = codes_pool.tile(
-                [P, TOKEN_TILES, ROUND_GROUPS, P], U32, name="x_codes", tag="x_codes", align_bytes=64
+                [P, ROUND_GROUPS, P], U32, name="x_codes", tag="x_codes", align_bytes=64
             )
             scales = codes_pool.tile(
-                [P, TOKEN_TILES, ROUND_GROUPS, P], U8, name="x_scales", tag="x_scales", align_bytes=64
+                [P, ROUND_GROUPS, P], U8, name="x_scales", tag="x_scales", align_bytes=64
             )
             nc.vector.quantize_mx(
-                out=codes[:].rearrange("p b g t -> p (b g t)").bitcast(FP8X4),
-                scales=scales[:].rearrange("p b g t -> p (b g t)"),
-                in_=grouped[:].rearrange("p b g t j -> p (b g t j)"),
+                out=codes[:].rearrange("p g t -> p (g t)").bitcast(FP8X4),
+                scales=scales[:].rearrange("p g t -> p (g t)"),
+                in_=x_grouped[unit][:].rearrange("p g t j -> p (g t j)"),
             )
-            x_codes[rnd] = codes
-            x_scales[rnd] = scales
+            x_codes[unit] = codes
+            x_scales[unit] = scales
 
         def multiply(rnd, branch):
             for piece in range(PIECES):
@@ -187,8 +182,8 @@ def tile_feedforward_pa_k_kernel(
                         chunk, in_plane = divmod(group, PLANE_GROUPS)
                         nc.tensor.matmul_mx(
                             out=acc[(branch, tt)][:],
-                            lhsT=x_codes[rnd][:, tt, local, :].bitcast(FP8X4),
-                            lhsT_scale=x_scales[rnd][:, tt, local, :],
+                            lhsT=x_codes[TOKEN_TILES * rnd + tt][:, local, :].bitcast(FP8X4),
+                            lhsT_scale=x_scales[TOKEN_TILES * rnd + tt][:, local, :],
                             rhs=w_pieces[(rnd, branch, piece)][:, i, :].bitcast(FP8X4),
                             rhs_scale=planes[(branch, chunk)][4 * chunk : P, in_plane, :],
                             start=(group == 0),
@@ -208,18 +203,22 @@ def tile_feedforward_pa_k_kernel(
         def multiply_lora():
             for branch in branches:
                 for tt in range(TOKEN_TILES):
-                    product = turn_psum.tile([P, F], F32, name="product", tag="turn")
+                    product = turn_psum.tile([P, PACK, P], F32, name="product", tag="turn")
                     nc.tensor.matmul(
-                        out=product[:],
+                        out=product[:].rearrange("s t p -> s (t p)"),
                         lhsT=lora_turned[branch][:, tt, :],
-                        rhs=lora_turned[branch][:, TOKEN_TILES:, :].rearrange("r j p -> r (j p)"),
+                        rhs=lora_turned[branch][:, TOKEN_TILES:, :].rearrange("r t p -> r (t p)"),
                         start=True,
                         stop=True,
                     )
                     lora_term[(branch, tt)] = keep.tile(
-                        [P, F], F32, name="lora_term_%s_%d" % (branch, tt)
+                        [P, PACK, P], F32, name="lora_term_%s_%d" % (branch, tt)
                     )
-                    nc.scalar.mul(out=lora_term[(branch, tt)][:], in_=product[:], mul=LORA_SCALING)
+                    nc.scalar.mul(
+                        out=lora_term[(branch, tt)][:],
+                        in_=product[:],
+                        mul=LORA_SCALING,
+                    )
 
         identity_f32 = keep.tile([P, P], F32, name="identity_f32")
         make_identity(nc, identity_f32[:])
@@ -234,31 +233,42 @@ def tile_feedforward_pa_k_kernel(
                 acc[(branch, tt)] = acc_psum.tile([P, F], F32, name="acc_%s_%d" % (branch, tt))
 
         zero_planes(0)
-        for rnd in range(2):
-            for tt in range(TOKEN_TILES):
-                load_x(rnd, tt)
-                load_scale_rows(nc.sync, I32, branches[rnd], 0, (2 * tt, 2 * tt + 1))
+        for unit in range(TOKEN_TILES):
+            load_x(unit)
+            load_scale_rows(nc.sync, I32, branches[unit], 0, range(4))
         zero_planes(1)
         for branch in branches:
             load_scale_rows(nc.gpsimd, F32, branch, 1, range(4))
-        load_w(0)
-        load_lora()
-        prepare_x(0)
+        load_x(2)
+        load_w(0, "w1")
+        load_x(3)
+        load_x(4)
+        load_w(0, "w3")
+        sort_x(0)
+        for unit in range(TOKEN_TILES):
+            sort_x(unit + 1)
+            turn_x(unit)
+            quantise_x(unit)
 
         a2_words = keep.tile([P, R], U32, name="a2_words", align_bytes=64)
         a2_plane = keep.tile([P, R], U8, name="a2_plane", align_bytes=64)
 
-        for rnd in range(ROUNDS):
-            if rnd + 2 < ROUNDS:
-                for tt in range(TOKEN_TILES):
-                    load_x(rnd + 2, tt)
+        for step in range(2 * ROUNDS):
+            rnd, odd = divmod(step, 2)
+            if step + 5 < 2 * ROUNDS:
+                load_x(step + 5)
             if rnd + 1 < ROUNDS:
-                load_w(rnd + 1)
-            if rnd == LORA_ROUND:
+                load_w(rnd + 1, branches[odd])
+            if step == 0:
+                load_lora()
+            if step == LORA_STEP:
                 transpose_lora()
-            if rnd + 1 < ROUNDS:
-                prepare_x(rnd + 1)
-            if rnd == 0:
+            if step + 3 < 2 * ROUNDS:
+                sort_x(step + 3)
+            if step + 2 < 2 * ROUNDS:
+                turn_x(step + 2)
+                quantise_x(step + 2)
+            if step == 1:
                 for chunk in range(2, GROUPS // PLANE_GROUPS):
                     zero_planes(chunk)
                     for branch in branches:
@@ -273,58 +283,63 @@ def tile_feedforward_pa_k_kernel(
                         out=a2_plane[r : P : 32, :].bitcast(F32),
                         in_=lora_A2_scales[0].bitcast(F32)[r : 16 : 4, :],
                     )
-            if rnd == LORA_ROUND:
+            if step == LORA_STEP:
                 multiply_lora()
-            multiply(rnd, "w1")
-            if rnd == ROUNDS - 1:
+            multiply(rnd, branches[odd])
+            if step == 2 * ROUNDS - 2:
                 for tt in range(TOKEN_TILES):
-                    h1 = keep.tile([P, F], F32, name="h1_%d" % tt)
+                    h1 = keep.tile([P, PACK, P], F32, name="h1_%d" % tt)
                     nc.vector.tensor_add(
-                        out=h1[:], in0=acc[("w1", tt)][:], in1=lora_term[("w1", tt)][:]
+                        out=h1[:],
+                        in0=acc[("w1", tt)][:].rearrange("s (p t) -> s t p", t=PACK),
+                        in1=lora_term[("w1", tt)][:],
                     )
-                    gate[tt] = keep.tile([P, F], F32, name="gate_%d" % tt)
+                    gate[tt] = keep.tile([P, PACK, P], F32, name="gate_%d" % tt)
                     nc.scalar.activation(out=gate[tt][:], in_=h1[:], func=SILU)
-            multiply(rnd, "w3")
 
         h3 = {}
         g_sorted = {}
         for tt in range(TOKEN_TILES):
-            h3[tt] = keep.tile([P, F], F32, name="h3_%d" % tt)
-            nc.vector.tensor_add(out=h3[tt][:], in0=acc[("w3", tt)][:], in1=lora_term[("w3", tt)][:])
-            g_sorted[tt] = keep.tile([P, PACK, P], BF16, name="g_sorted_%d" % tt)
-            nc.vector.tensor_mul(
-                out=g_sorted[tt][:],
-                in0=h3[tt][:].rearrange("s (p t) -> s t p", t=PACK),
-                in1=gate[tt][:].rearrange("s (p t) -> s t p", t=PACK),
+            h3[tt] = keep.tile([P, PACK, P], F32, name="h3_%d" % tt)
+            nc.vector.tensor_add(
+                out=h3[tt][:],
+                in0=acc[("w3", tt)][:].rearrange("s (p t) -> s t p", t=PACK),
+                in1=lora_term[("w3", tt)][:],
             )
-        g_grouped = keep.tile([P, TOKEN_TILES, P, PACK], BF16, name="g_grouped", align_bytes=64)
+            g_sorted[tt] = keep.tile([P, PACK, P], BF16, name="g_sorted_%d" % tt)
+            nc.vector.tensor_mul(out=g_sorted[tt][:], in0=h3[tt][:], in1=gate[tt][:])
+        g_grouped = {}
         for tt in range(TOKEN_TILES):
             g_turned = turn_psum.tile([P, PACK, P], BF16, name="g_turned", tag="turn")
             for t in range(PACK):
                 nc.tensor.transpose(g_turned[:, t, :], g_sorted[tt][:, t, :], identity_bf16[:])
-            nc.scalar.copy(out=g_grouped[:, tt, :, :], in_=g_turned[:].rearrange("p t s -> p s t"))
+            g_grouped[tt] = keep.tile([P, P, PACK], BF16, name="g_grouped_%d" % tt, align_bytes=64)
+            nc.scalar.copy(out=g_grouped[tt][:], in_=g_turned[:].rearrange("p t s -> p s t"))
         for tt in range(TOKEN_TILES):
-            g = keep.tile([P, F], F32, name="g_%d" % tt)
-            nc.vector.tensor_mul(out=g[:], in0=h3[tt][:], in1=gate[tt][:])
-            nc.sync.dma_start(out=out_0[tt], in_=g[:])
-        g_codes = keep.tile([P, TOKEN_TILES, P], U32, name="g_codes", align_bytes=64)
-        g_scales = keep.tile([P, TOKEN_TILES, P], U8, name="g_scales", align_bytes=64)
-        nc.vector.quantize_mx(
-            out=g_codes[:].rearrange("p b s -> p (b s)").bitcast(FP8X4),
-            scales=g_scales[:].rearrange("p b s -> p (b s)"),
-            in_=g_grouped[:].rearrange("p b s t -> p (b s t)"),
-        )
-        ga2_psum = turn_psum.tile([P, TOKEN_TILES, R], F32, name="ga2_psum", tag="turn")
-        for tt in range(TOKEN_TILES):
+            g_codes = keep.tile([P, P], U32, name="g_codes_%d" % tt, align_bytes=64)
+            g_scales = keep.tile([P, P], U8, name="g_scales_%d" % tt, align_bytes=64)
+            nc.vector.quantize_mx(
+                out=g_codes[:].bitcast(FP8X4),
+                scales=g_scales[:],
+                in_=g_grouped[tt][:].rearrange("p s t -> p (s t)"),
+            )
+            ga2_psum = turn_psum.tile([P, R], F32, name="ga2_psum", tag="turn")
             nc.tensor.matmul_mx(
-                out=ga2_psum[:, tt, :],
-                lhsT=g_codes[:, tt, :].bitcast(FP8X4),
-                lhsT_scale=g_scales[:, tt, :],
+                out=ga2_psum[:],
+                lhsT=g_codes[:].bitcast(FP8X4),
+                lhsT_scale=g_scales[:],
                 rhs=a2_words[:].bitcast(FP8X4),
                 rhs_scale=a2_plane[:],
                 start=True,
                 stop=True,
             )
-        ga2 = keep.tile([P, TOKEN_TILES, R], F32, name="ga2")
-        nc.scalar.copy(out=ga2[:], in_=ga2_psum[:])
-        nc.sync.dma_start(out=out_1.rearrange("b s r -> s b r"), in_=ga2[:])
+            ga2 = keep.tile([P, R], F32, name="ga2_%d" % tt)
+            nc.scalar.copy(out=ga2[:], in_=ga2_psum[:])
+            nc.scalar.dma_start(out=out_1[tt], in_=ga2[:])
+            g = keep.tile([P, F], F32, name="g_%d" % tt)
+            nc.vector.tensor_mul(
+                out=g[:].rearrange("s (p t) -> s p t", t=PACK),
+                in0=h3[tt][:].rearrange("s t p -> s p t"),
+                in1=gate[tt][:].rearrange("s t p -> s p t"),
+            )
+            nc.sync.dma_start(out=out_0[tt], in_=g[:])

@@ -86,26 +86,30 @@ def tile_feedforward_pa_k_kernel(
             x_raw[unit] = raw
 
         def load_w(rnd, branch):
+            last = rnd == ROUNDS - 1 and branch == branches[-1]
+            split = PIECE_GROUPS if last else 1
             for piece in range(PIECES):
                 first = rnd * ROUND_GROUPS + piece * PIECE_GROUPS
                 w_piece = w_pool.tile(
                     [P, PIECE_GROUPS, F], U32, name="w_piece", tag="w_piece", align_bytes=64
                 )
-                nc.sync.dma_start(
-                    out=w_piece[:].bitcast(I32),
-                    in_=words_of[branch][first : first + PIECE_GROUPS]
-                    .rearrange("g p n t -> p g (n t)")
-                    .bitcast(I32),
-                )
+                count = PIECE_GROUPS // split
+                for i in range(split):
+                    nc.sync.dma_start(
+                        out=w_piece[:, i * count : (i + 1) * count, :].bitcast(I32),
+                        in_=words_of[branch][first + i * count : first + (i + 1) * count]
+                        .rearrange("g p n t -> p g (n t)")
+                        .bitcast(I32),
+                    )
                 w_pieces[(rnd, branch, piece)] = w_piece
 
-        def load_scale_rows(queue, view, branch, chunk, rows):
-            source = scales_of[branch].bitcast(view)[
+        def load_scale_rows(branch, chunk):
+            source = scales_of[branch].bitcast(F32)[
                 chunk * PLANE_GROUPS : (chunk + 1) * PLANE_GROUPS
             ]
-            for r in rows:
-                queue.dma_start(
-                    out=planes[(branch, chunk)][4 * chunk + r : P : 32, :, :].bitcast(view),
+            for r in range(4):
+                nc.gpsimd.dma_start(
+                    out=planes[(branch, chunk)][4 * chunk + r : P : 32, :, :].bitcast(F32),
                     in_=source[:, r : 16 : 4, :].rearrange("g q n -> q g n"),
                 )
 
@@ -220,8 +224,11 @@ def tile_feedforward_pa_k_kernel(
                         mul=LORA_SCALING,
                     )
 
+        zero_planes(0)
         identity_f32 = keep.tile([P, P], F32, name="identity_f32")
         make_identity(nc, identity_f32[:])
+        for branch in branches:
+            load_scale_rows(branch, 0)
         identity_bf16 = keep.tile([P, P], BF16, name="identity_bf16")
         make_identity(nc, identity_bf16[:])
         table_in = keep.tile([P, 1], F32, name="table_in")
@@ -232,13 +239,11 @@ def tile_feedforward_pa_k_kernel(
             for tt in range(TOKEN_TILES):
                 acc[(branch, tt)] = acc_psum.tile([P, F], F32, name="acc_%s_%d" % (branch, tt))
 
-        zero_planes(0)
         for unit in range(TOKEN_TILES):
             load_x(unit)
-            load_scale_rows(nc.sync, I32, branches[unit], 0, range(4))
         zero_planes(1)
         for branch in branches:
-            load_scale_rows(nc.gpsimd, F32, branch, 1, range(4))
+            load_scale_rows(branch, 1)
         load_x(2)
         load_w(0, "w1")
         load_x(3)
@@ -272,7 +277,7 @@ def tile_feedforward_pa_k_kernel(
                 for chunk in range(2, GROUPS // PLANE_GROUPS):
                     zero_planes(chunk)
                     for branch in branches:
-                        load_scale_rows(nc.gpsimd, F32, branch, chunk, range(4))
+                        load_scale_rows(branch, chunk)
                 nc.vector.memset(a2_plane[:].bitcast(I32), 0)
                 nc.gpsimd.dma_start(
                     out=a2_words[:].bitcast(F32),
@@ -306,6 +311,7 @@ def tile_feedforward_pa_k_kernel(
                 in0=acc[("w3", tt)][:].rearrange("s (p t) -> s t p", t=PACK),
                 in1=lora_term[("w3", tt)][:],
             )
+        for tt in range(TOKEN_TILES):
             g_sorted[tt] = keep.tile([P, PACK, P], BF16, name="g_sorted_%d" % tt)
             nc.vector.tensor_mul(out=g_sorted[tt][:], in0=h3[tt][:], in1=gate[tt][:])
         g_grouped = {}
@@ -315,7 +321,17 @@ def tile_feedforward_pa_k_kernel(
                 nc.tensor.transpose(g_turned[:, t, :], g_sorted[tt][:, t, :], identity_bf16[:])
             g_grouped[tt] = keep.tile([P, P, PACK], BF16, name="g_grouped_%d" % tt, align_bytes=64)
             nc.scalar.copy(out=g_grouped[tt][:], in_=g_turned[:].rearrange("p t s -> p s t"))
-        for tt in range(TOKEN_TILES):
+
+        def store_g(tt):
+            g = keep.tile([P, F], F32, name="g_%d" % tt)
+            nc.vector.tensor_mul(
+                out=g[:].rearrange("s (p t) -> s p t", t=PACK),
+                in0=h3[tt][:].rearrange("s t p -> s p t"),
+                in1=gate[tt][:].rearrange("s t p -> s p t"),
+            )
+            nc.sync.dma_start(out=out_0[tt], in_=g[:])
+
+        def project_g(tt):
             g_codes = keep.tile([P, P], U32, name="g_codes_%d" % tt, align_bytes=64)
             g_scales = keep.tile([P, P], U8, name="g_scales_%d" % tt, align_bytes=64)
             nc.vector.quantize_mx(
@@ -336,10 +352,8 @@ def tile_feedforward_pa_k_kernel(
             ga2 = keep.tile([P, R], F32, name="ga2_%d" % tt)
             nc.scalar.copy(out=ga2[:], in_=ga2_psum[:])
             nc.scalar.dma_start(out=out_1[tt], in_=ga2[:])
-            g = keep.tile([P, F], F32, name="g_%d" % tt)
-            nc.vector.tensor_mul(
-                out=g[:].rearrange("s (p t) -> s p t", t=PACK),
-                in0=h3[tt][:].rearrange("s t p -> s p t"),
-                in1=gate[tt][:].rearrange("s t p -> s p t"),
-            )
-            nc.sync.dma_start(out=out_0[tt], in_=g[:])
+
+        store_g(0)
+        project_g(0)
+        project_g(1)
+        store_g(1)

from contextlib import ExitStack

import concourse.mybir as mybir
from concourse.masks import make_identity

F32 = mybir.dt.float32
BF16 = mybir.dt.bfloat16
I32 = mybir.dt.int32
U32 = mybir.dt.uint32
U8 = mybir.dt.uint8
FP8X4 = mybir.dt.float8_e4m3fn_x4
SILU = mybir.ActivationFunctionType.Silu

P = 128
TOKEN_TILES = 2
D = 16384
F = 512
R = 128
PACK = 4
K_PASS = P * PACK
GROUPS = D // K_PASS
ROUND_GROUPS = 4
ROUNDS = GROUPS // ROUND_GROUPS
ROUND_COLS = K_PASS * ROUND_GROUPS
PIECE_GROUPS = 2
PIECES = ROUND_GROUPS // PIECE_GROUPS
BANK_GROUPS = 2
PLANE_GROUPS = 8
LORA_STEP = 3
LORA_BLOCKS = TOKEN_TILES + F // P
LORA_SCALING = 2.0

FLOPS = 2 * TOKEN_TILES * P * (2 * D * F + 2 * R * F + F * R)


def tile_feedforward_pa_k_kernel(
    tc,
    x,
    w1_words,
    w1_scales,
    w3_words,
    w3_scales,
    xa1,
    xa3,
    lora_B1,
    lora_B3,
    lora_A2_words,
    lora_A2_scales,
    out_0,
    out_1,
):
    nc = tc.nc
    branches = ("w1", "w3")
    words_of = {"w1": w1_words, "w3": w3_words}
    scales_of = {"w1": w1_scales, "w3": w3_scales}
    lora_inputs = {"w1": (xa1, lora_B1), "w3": (xa3, lora_B3)}

    with ExitStack() as ctx:
        keep = ctx.enter_context(tc.tile_pool(name="keep", bufs=1))
        x_pool = ctx.enter_context(tc.tile_pool(name="x_pool", bufs=4 * TOKEN_TILES))
        sorted_pool = ctx.enter_context(tc.tile_pool(name="sorted_pool", bufs=3))
        grouped_pool = ctx.enter_context(tc.tile_pool(name="grouped_pool", bufs=3))
        codes_pool = ctx.enter_context(tc.tile_pool(name="codes_pool", bufs=6))
        w_pool = ctx.enter_context(tc.tile_pool(name="w_pool", bufs=4 * 2 * PIECES))
        turn_psum = ctx.enter_context(tc.psum_pool(name="turn_psum", bufs=4))
        acc_psum = ctx.enter_context(tc.psum_pool(name="acc_psum", bufs=1))
        ctx.enter_context(tc.manual_schedule())

        x_raw = {}
        x_sorted = {}
        x_grouped = {}
        x_codes = {}
        x_scales = {}
        w_pieces = {}
        planes = {}
        lora_in = {}
        lora_turned = {}
        lora_term = {}
        acc = {}
        gate = {}

        def load_x(unit):
            rnd, tt = divmod(unit, TOKEN_TILES)
            raw = x_pool.tile([P, ROUND_COLS], BF16, name="x_raw", tag="x_raw")
            nc.sync.dma_start(out=raw[:], in_=x[tt, :, rnd * ROUND_COLS : (rnd + 1) * ROUND_COLS])
            x_raw[unit] = raw

        def load_w(rnd, branch):
            last = rnd == ROUNDS - 1 and branch == branches[-1]
            split = PIECE_GROUPS if last else 1
            for piece in range(PIECES):
                first = rnd * ROUND_GROUPS + piece * PIECE_GROUPS
                w_piece = w_pool.tile(
                    [P, PIECE_GROUPS, F], U32, name="w_piece", tag="w_piece", align_bytes=64
                )
                count = PIECE_GROUPS // split
                for i in range(split):
                    nc.sync.dma_start(
                        out=w_piece[:, i * count : (i + 1) * count, :].bitcast(I32),
                        in_=words_of[branch][first + i * count : first + (i + 1) * count]
                        .rearrange("g p n t -> p g (n t)")
                        .bitcast(I32),
                    )
                w_pieces[(rnd, branch, piece)] = w_piece

        def load_scale_rows(branch, chunk):
            source = scales_of[branch].bitcast(F32)[
                chunk * PLANE_GROUPS : (chunk + 1) * PLANE_GROUPS
            ]
            for r in range(4):
                nc.gpsimd.dma_start(
                    out=planes[(branch, chunk)][4 * chunk + r : P : 32, :, :].bitcast(F32),
                    in_=source[:, r : 16 : 4, :].rearrange("g q n -> q g n"),
                )

        def zero_planes(chunk):
            for branch in branches:
                planes[(branch, chunk)] = keep.tile(
                    [P, PLANE_GROUPS, F], U8, name="planes_%s_%d" % (branch, chunk), align_bytes=64
                )
                nc.vector.memset(planes[(branch, chunk)][:].bitcast(I32), 0)

        def load_lora():
            for branch in branches:
                xa, lora_b = lora_inputs[branch]
                lora_in[branch] = keep.tile([P, LORA_BLOCKS, R], BF16, name="lora_in_" + branch)
                nc.sync.dma_start(
                    out=lora_in[branch][:, 0:TOKEN_TILES, :], in_=xa.rearrange("b s r -> s b r")
                )
                nc.sync.dma_start(
                    out=lora_in[branch][:, TOKEN_TILES:, :],
                    in_=lora_b.rearrange("(p t) r -> p t r", t=PACK),
                )

        def sort_x(unit):
            x_sorted[unit] = sorted_pool.tile(
                [P, ROUND_GROUPS, 2, P], F32, name="sorted_words", tag="sorted_words"
            )
            nc.vector.tensor_copy(
                out=x_sorted[unit][:],
                in_=x_raw[unit][:].bitcast(F32).rearrange("s (g p u) -> s g u p", g=ROUND_GROUPS, u=2),
            )

        def turn_x(unit):
            grouped = grouped_pool.tile(
                [P, ROUND_GROUPS, P, PACK], BF16, name="grouped", tag="grouped", align_bytes=64
            )
            grouped_words = grouped[:].bitcast(F32)
            for bank in range(ROUND_GROUPS // BANK_GROUPS):
                turned = turn_psum.tile([P, BANK_GROUPS, 2, P], F32, name="turned", tag="turn")
                for i in range(BANK_GROUPS):
                    for u in range(2):
                        nc.tensor.transpose(
                            turned[:, i, u, :],
                            x_sorted[unit][:, bank * BANK_GROUPS + i, u, :],
                            identity_f32[:],
                        )
                copy_out = nc.scalar.copy if bank % 2 == 0 else nc.vector.tensor_copy
                copy_out(
                    out=grouped_words[:, bank * BANK_GROUPS : (bank + 1) * BANK_GROUPS, :, :],
                    in_=turned[:].rearrange("p g u t -> p g t u"),
                )
            x_grouped[unit] = grouped

        def quantise_x(unit):
            codes = codes_pool.tile(
                [P, ROUND_GROUPS, P], U32, name="x_codes", tag="x_codes", align_bytes=64
            )
            scales = codes_pool.tile(
                [P, ROUND_GROUPS, P], U8, name="x_scales", tag="x_scales", align_bytes=64
            )
            nc.vector.quantize_mx(
                out=codes[:].rearrange("p g t -> p (g t)").bitcast(FP8X4),
                scales=scales[:].rearrange("p g t -> p (g t)"),
                in_=x_grouped[unit][:].rearrange("p g t j -> p (g t j)"),
            )
            x_codes[unit] = codes
            x_scales[unit] = scales

        def multiply(rnd, branch):
            for piece in range(PIECES):
                for tt in range(TOKEN_TILES):
                    for i in range(PIECE_GROUPS):
                        local = piece * PIECE_GROUPS + i
                        group = rnd * ROUND_GROUPS + local
                        chunk, in_plane = divmod(group, PLANE_GROUPS)
                        nc.tensor.matmul_mx(
                            out=acc[(branch, tt)][:],
                            lhsT=x_codes[TOKEN_TILES * rnd + tt][:, local, :].bitcast(FP8X4),
                            lhsT_scale=x_scales[TOKEN_TILES * rnd + tt][:, local, :],
                            rhs=w_pieces[(rnd, branch, piece)][:, i, :].bitcast(FP8X4),
                            rhs_scale=planes[(branch, chunk)][4 * chunk : P, in_plane, :],
                            start=(group == 0),
                            stop=(group == GROUPS - 1),
                        )

        def transpose_lora():
            for branch in branches:
                turned = turn_psum.tile([P, LORA_BLOCKS, P], BF16, name="lora_ps", tag="turn")
                for i in range(LORA_BLOCKS):
                    nc.tensor.transpose(turned[:, i, :], lora_in[branch][:, i, :], identity_bf16[:])
                lora_turned[branch] = keep.tile(
                    [P, LORA_BLOCKS, P], BF16, name="lora_turned_" + branch
                )
                nc.scalar.copy(out=lora_turned[branch][:], in_=turned[:])

        def multiply_lora():
            for branch in branches:
                for tt in range(TOKEN_TILES):
                    product = turn_psum.tile([P, PACK, P], F32, name="product", tag="turn")
                    nc.tensor.matmul(
                        out=product[:].rearrange("s t p -> s (t p)"),
                        lhsT=lora_turned[branch][:, tt, :],
                        rhs=lora_turned[branch][:, TOKEN_TILES:, :].rearrange("r t p -> r (t p)"),
                        start=True,
                        stop=True,
                    )
                    lora_term[(branch, tt)] = keep.tile(
                        [P, PACK, P], F32, name="lora_term_%s_%d" % (branch, tt)
                    )
                    nc.scalar.mul(
                        out=lora_term[(branch, tt)][:],
                        in_=product[:],
                        mul=LORA_SCALING,
                    )

        zero_planes(0)
        identity_f32 = keep.tile([P, P], F32, name="identity_f32")
        make_identity(nc, identity_f32[:])
        for branch in branches:
            load_scale_rows(branch, 0)
        identity_bf16 = keep.tile([P, P], BF16, name="identity_bf16")
        make_identity(nc, identity_bf16[:])
        table_in = keep.tile([P, 1], F32, name="table_in")
        table_out = keep.tile([P, 1], F32, name="table_out")
        nc.vector.memset(table_in[:], 0.0)
        nc.scalar.activation(out=table_out[:], in_=table_in[:], func=SILU)
        for branch in branches:
            for tt in range(TOKEN_TILES):
                acc[(branch, tt)] = acc_psum.tile([P, F], F32, name="acc_%s_%d" % (branch, tt))

        for unit in range(TOKEN_TILES):
            load_x(unit)
        zero_planes(1)
        for branch in branches:
            load_scale_rows(branch, 1)
        load_x(2)
        load_w(0, "w1")
        load_x(3)
        load_x(4)
        load_w(0, "w3")
        sort_x(0)
        for unit in range(TOKEN_TILES):
            sort_x(unit + 1)
            turn_x(unit)
            quantise_x(unit)

        a2_words = keep.tile([P, R], U32, name="a2_words", align_bytes=64)
        a2_plane = keep.tile([P, R], U8, name="a2_plane", align_bytes=64)

        for step in range(2 * ROUNDS):
            rnd, odd = divmod(step, 2)
            if step + 5 < 2 * ROUNDS:
                load_x(step + 5)
            if rnd + 1 < ROUNDS:
                load_w(rnd + 1, branches[odd])
            if step == 0:
                load_lora()
            if step == LORA_STEP:
                transpose_lora()
            if step + 3 < 2 * ROUNDS:
                sort_x(step + 3)
            if step + 2 < 2 * ROUNDS:
                turn_x(step + 2)
                quantise_x(step + 2)
            if step == 1:
                for chunk in range(2, GROUPS // PLANE_GROUPS):
                    zero_planes(chunk)
                    for branch in branches:
                        load_scale_rows(branch, chunk)
                nc.vector.memset(a2_plane[:].bitcast(I32), 0)
                nc.gpsimd.dma_start(
                    out=a2_words[:].bitcast(F32),
                    in_=lora_A2_words[0].rearrange("p n t -> p (n t)").bitcast(F32),
                )
                for r in range(4):
                    nc.gpsimd.dma_start(
                        out=a2_plane[r : P : 32, :].bitcast(F32),
                        in_=lora_A2_scales[0].bitcast(F32)[r : 16 : 4, :],
                    )
            if step == LORA_STEP:
                multiply_lora()
            multiply(rnd, branches[odd])
            if step == 2 * ROUNDS - 2:
                for tt in range(TOKEN_TILES):
                    h1 = keep.tile([P, PACK, P], F32, name="h1_%d" % tt)
                    nc.vector.tensor_add(
                        out=h1[:],
                        in0=acc[("w1", tt)][:].rearrange("s (p t) -> s t p", t=PACK),
                        in1=lora_term[("w1", tt)][:],
                    )
                    gate[tt] = keep.tile([P, PACK, P], F32, name="gate_%d" % tt)
                    nc.scalar.activation(out=gate[tt][:], in_=h1[:], func=SILU)

        h3 = {}
        g_sorted = {}
        for tt in range(TOKEN_TILES):
            h3[tt] = keep.tile([P, PACK, P], F32, name="h3_%d" % tt)
            nc.vector.tensor_add(
                out=h3[tt][:],
                in0=acc[("w3", tt)][:].rearrange("s (p t) -> s t p", t=PACK),
                in1=lora_term[("w3", tt)][:],
            )
        for tt in range(TOKEN_TILES):
            g_sorted[tt] = keep.tile([P, PACK, P], BF16, name="g_sorted_%d" % tt)
            nc.vector.tensor_mul(out=g_sorted[tt][:], in0=h3[tt][:], in1=gate[tt][:])
        g_grouped = {}
        for tt in range(TOKEN_TILES):
            g_turned = turn_psum.tile([P, PACK, P], BF16, name="g_turned", tag="turn")
            for t in range(PACK):
                nc.tensor.transpose(g_turned[:, t, :], g_sorted[tt][:, t, :], identity_bf16[:])
            g_grouped[tt] = keep.tile([P, P, PACK], BF16, name="g_grouped_%d" % tt, align_bytes=64)
            nc.scalar.copy(out=g_grouped[tt][:], in_=g_turned[:].rearrange("p t s -> p s t"))

        def store_g(tt):
            g = keep.tile([P, F], F32, name="g_%d" % tt)
            nc.vector.tensor_mul(
                out=g[:].rearrange("s (p t) -> s p t", t=PACK),
                in0=h3[tt][:].rearrange("s t p -> s p t"),
                in1=gate[tt][:].rearrange("s t p -> s p t"),
            )
            nc.sync.dma_start(out=out_0[tt], in_=g[:])

        def project_g(tt):
            g_codes = keep.tile([P, P], U32, name="g_codes_%d" % tt, align_bytes=64)
            g_scales = keep.tile([P, P], U8, name="g_scales_%d" % tt, align_bytes=64)
            nc.vector.quantize_mx(
                out=g_codes[:].bitcast(FP8X4),
                scales=g_scales[:],
                in_=g_grouped[tt][:].rearrange("p s t -> p (s t)"),
            )
            ga2_psum = turn_psum.tile([P, R], F32, name="ga2_psum", tag="turn")
            nc.tensor.matmul_mx(
                out=ga2_psum[:],
                lhsT=g_codes[:].bitcast(FP8X4),
                lhsT_scale=g_scales[:],
                rhs=a2_words[:].bitcast(FP8X4),
                rhs_scale=a2_plane[:],
                start=True,
                stop=True,
            )
            ga2 = keep.tile([P, R], F32, name="ga2_%d" % tt)
            nc.scalar.copy(out=ga2[:], in_=ga2_psum[:])
            nc.scalar.dma_start(out=out_1[tt], in_=ga2[:])

        store_g(0)
        project_g(0)
        project_g(1)
        store_g(1)
